import numpy as np
import ml_dtypes


def mxq(x, axis, fmt="e4m3"):
    dtype, down = {"e4m3": (ml_dtypes.float8_e4m3fn, 7), "e5m2": (ml_dtypes.float8_e5m2, 14)}[fmt]
    v = np.moveaxis(np.asarray(x, np.float32).astype(ml_dtypes.bfloat16).astype(np.float64), axis, -1)
    blocks = v.reshape(v.shape[:-1] + (-1, 32))
    amax = np.abs(blocks).max(-1, keepdims=True)
    byte = np.maximum(np.where(amax > 0, np.frexp(amax)[1] - 1 + 127, 0) - down, 1)
    scale = np.exp2(byte - 127.0)
    codes = (blocks / scale).astype(np.float32).astype(dtype).astype(np.float64)
    return np.moveaxis((codes * scale).reshape(v.shape), -1, axis)


WIDE = False


def mx_kscale(k):
    if not WIDE:
        return np.ones(k)
    levels = np.array([10, -10, 5, -5, 0])
    a = np.random.permutation(np.resize(levels, k // 512 * 4)).reshape(k // 512, 4)
    idx = np.arange(k)
    return np.exp2(a[idx // 512, idx % 128 // 32])


BF16 = ml_dtypes.bfloat16


def bf(x):
    return np.asarray(x, np.float32).astype(BF16)


def f64(x):
    return np.asarray(x).astype(np.float64)


B, HQ, HKV, S, D, W = 1, 4, 1, 2048, 128, 256
SCALE = 1.0 / np.sqrt(D)
WINDOW_RIGHT = 0
SOFTCAP = 30.0
EPS = 1e-9
MXB = 32
Q0 = 8.0


def setup_inputs():
    lv = np.unique(mx_kscale(S))
    t = np.tile(np.repeat(lv[np.arange(W // MXB) % len(lv)], MXB), S // W)
    Q = np.random.standard_normal((B, HQ, S, D)) * 1.5
    K = np.random.standard_normal((B, HKV, S, D)) * 1.5
    V = np.random.standard_normal((B, HKV, S, D))
    Q[..., 0] = Q0
    K[..., 0] += SOFTCAP * np.arctanh(-np.log(t) / SOFTCAP) / (Q0 * SCALE)
    V = V * (t / t.min())[:, None]
    return {"Q": bf(Q), "K": bf(K), "V": bf(V)}


def reference(Q, K, V):
    G = HQ // HKV
    Qf = f64(Q).reshape(B, HKV, G, S, D)
    Kf = f64(K)
    Vf = f64(V)
    s = (Qf @ Kf.transpose(0, 1, 3, 2)[:, :, None]) * SCALE
    s = SOFTCAP * np.tanh(s / SOFTCAP)
    sq, sk = Qf.shape[3], Kf.shape[2]
    shift = sk - sq
    iq = np.arange(sq)[:, None]
    jk = np.arange(sk)[None, :]
    valid = np.ones((sq, sk), dtype=bool)
    valid &= jk <= iq + shift
    valid &= jk >= iq + shift - W
    valid &= jk <= iq + shift + WINDOW_RIGHT
    s = np.where(valid, s, -np.inf)
    m = s.max(-1, keepdims=True)
    m = np.where(np.isfinite(m), m, 0.0)
    p = np.exp(s - m)
    l = p.sum(-1, keepdims=True)
    o = (mxq(p, 4, "e4m3") @ mxq(Vf, 2, "e4m3")[:, :, None]) / (l + EPS)
    return o.reshape(B, HQ, S, D)

@@ -1,0 +1,274 @@
+from contextlib import ExitStack
+
+import concourse.mybir as mybir
+from concourse.masks import make_identity
+
+BF16 = mybir.dt.bfloat16
+F32 = mybir.dt.float32
+U32 = mybir.dt.uint32
+U8 = mybir.dt.uint8
+I32 = mybir.dt.int32
+FP8X4 = mybir.dt.float8_e4m3fn_x4
+ACT = mybir.ActivationFunctionType
+ALU = mybir.AluOpType
+AX = mybir.AxisListType
+
+P = 128
+H = 4
+S = 2048
+D = 128
+WIN = 256
+QB = 32
+NT = S // QB
+TB = 4
+NB = NT // TB
+NG = (WIN + QB) // 32
+CW = 8 * NG
+SOFTCAP = 30.0
+SCALE = 1.0 / (128.0 ** 0.5)
+EPS = 1e-9
+FILL = -10000.0
+NV = 7
+
+FLOPS = 4 * H * D * (S * (WIN + 1) - WIN * (WIN + 1) // 2)
+
+ACT_COPIES = (1, 0, 1, 1, 0, 1, 0, 1)
+
+
+def tile_modelnew_kernel(tc, Q, K, V, out):
+    nc = tc.nc
+    with ExitStack() as ctx:
+        const = ctx.enter_context(tc.tile_pool(name="const", bufs=1))
+        tbp = ctx.enter_context(tc.tile_pool(name="tbp", bufs=4))
+        small = ctx.enter_context(tc.tile_pool(name="small", bufs=6))
+        gp = ctx.enter_context(tc.tile_pool(name="gp", bufs=3))
+        op = ctx.enter_context(tc.tile_pool(name="op", bufs=4))
+        ps_s = ctx.enter_context(tc.psum_pool(name="ps_s", bufs=3))
+        ps_t = ctx.enter_context(tc.psum_pool(name="ps_t", bufs=3))
+        ps_o = ctx.enter_context(tc.psum_pool(name="ps_o", bufs=2))
+
+        k_sb = const.tile([P, 4, 4, D], BF16)
+        q_sb = const.tile([P, NT, D], BF16)
+        v_raw = const.tile([P, NV, 4, D], BF16)
+        v_grp = const.tile([P, NV, D, 4], BF16, align_bytes=64)
+        v_w = const.tile([P, NV * D], U32, align_bytes=64)
+        v_s = const.tile([P, NV * D], U8, align_bytes=64)
+        kt = const.tile([P, S // 32, 4, 8], BF16)
+        qt = const.tile([P, NT, P], BF16)
+        pb0 = const.tile([P, 8, 4, P], BF16)
+        pb1 = const.tile([P, 8, 4, P], BF16)
+        ident = const.tile([P, P], BF16)
+
+        nc.vector.memset(pb0[:].bitcast(I32), 0)
+        nc.vector.memset(pb1[:].bitcast(I32), 0)
+        make_identity(nc, ident[:])
+
+        def load_k(g):
+            nc.sync.dma_start(
+                out=k_sb[:, g, :, :],
+                in_=K[0, 0, 512 * g : 512 * (g + 1), :].rearrange("(c t) d -> c t d", t=4),
+            )
+
+        def load_q(t0, t1):
+            for h in range(H):
+                nc.sync.dma_start(
+                    out=q_sb[h:P:H, t0:t1, :],
+                    in_=Q[0, h, QB * t0 : QB * t1, :].rearrange("(n q) d -> q n d", q=QB),
+                )
+
+        load_k(0)
+        load_q(0, 8)
+        load_k(1)
+        load_q(8, 16)
+        load_k(2)
+        load_k(3)
+        load_q(16, 32)
+        load_q(32, 64)
+        for v in range(NV):
+            nc.scalar.dma_start(
+                out=v_raw[:, v, :, :],
+                in_=V[0, 0, 256 * v : 256 * v + 512, :].rearrange("(p t) d -> p t d", t=4),
+            )
+
+        def k_transposes(g0):
+            tp = ps_t.tile([P, 1024], BF16, tag="tp")
+            for g in range(2):
+                for t in range(4):
+                    n = 4 * g + t
+                    nc.tensor.transpose(tp[:, P * n : P * (n + 1)], k_sb[:, g0 + g, t, :], ident[:])
+            for g in range(2):
+                nc.vector.tensor_copy(
+                    out=kt[:, 16 * (g0 + g) : 16 * (g0 + g + 1), :, :],
+                    in_=tp[:, 512 * g : 512 * (g + 1)].rearrange("d (t l e) -> d l t e", t=4, e=8),
+                )
+
+        def q_transposes(n8):
+            tp = ps_t.tile([P, 1024], BF16, tag="tp")
+            for n in range(8):
+                nc.tensor.transpose(tp[:, P * n : P * (n + 1)], q_sb[:, 8 * n8 + n, :], ident[:])
+            nc.vector.tensor_copy(
+                out=qt[:, 8 * n8 : 8 * (n8 + 1), :].rearrange("d n p -> d (n p)"), in_=tp[:]
+            )
+
+        def v_prep(v0, v1):
+            nc.vector.tensor_copy(
+                out=v_grp[:, v0:v1, :, :],
+                in_=v_raw[:, v0:v1, :, :].rearrange("p v t d -> p v d t"),
+            )
+
+        def v_quant(v0, v1):
+            nc.vector.quantize_mx(
+                out=v_w[:, D * v0 : D * v1].bitcast(FP8X4),
+                scales=v_s[:, D * v0 : D * v1],
+                in_=v_grp[:, v0:v1, :, :].rearrange("p v d t -> p (v d t)"),
+            )
+
+        state = {}
+        kt_flat = kt[:].rearrange("d l t e -> d (l t e)")
+
+        def stage_a(b):
+            tb = tbp.tile([P, NG, TB, 32], F32, tag="tb")
+            mt = small.tile([P, TB], F32, tag="mt")
+            nb = small.tile([P, TB], F32, tag="nb")
+            first = b < 2
+            for i in range(TB):
+                n = TB * b + i
+                lo = max(0, 8 - n)
+                sc = ps_s.tile([P, NG, 32], F32, tag="sc")
+                nc.tensor.matmul(
+                    out=sc[:, lo:NG, :].rearrange("p g e -> p (g e)"),
+                    lhsT=qt[:, n, :],
+                    rhs=kt_flat[:, 32 * (n - 8 + lo) : 32 * (n + 1)],
+                    start=True,
+                    stop=True,
+                )
+                nc.scalar.activation(
+                    out=tb[:, lo:NG, i, :], in_=sc[:, lo:NG, :], func=ACT.Tanh, scale=SCALE / SOFTCAP
+                )
+            if not first:
+                nc.gpsimd.affine_select(
+                    out=tb[:, 0, :, :].rearrange("p i e -> p (i e)"),
+                    in_=tb[:, 0, :, :].rearrange("p i e -> p (i e)"),
+                    pattern=[[0, TB], [4, 4], [16, 8]],
+                    compare_op=ALU.is_ge,
+                    fill=FILL,
+                    base=3,
+                    channel_multiplier=-1,
+                )
+            nc.gpsimd.affine_select(
+                out=tb[:, NG - 1, :, :].rearrange("p i e -> p (i e)"),
+                in_=tb[:, NG - 1, :, :].rearrange("p i e -> p (i e)"),
+                pattern=[[0, TB], [-4, 4], [-16, 8]],
+                compare_op=ALU.is_ge,
+                fill=FILL,
+                base=0,
+                channel_multiplier=1,
+            )
+            if first:
+                for i in range(TB):
+                    lo = max(0, 8 - (TB * b + i))
+                    nc.vector.tensor_reduce(
+                        out=mt[:, i : i + 1], in_=tb[:, lo:NG, i, :], axis=AX.XY, op=ALU.max
+                    )
+            else:
+                nc.vector.tensor_reduce(
+                    out=mt[:], in_=tb[:].rearrange("p g i e -> p i g e"), axis=AX.XY, op=ALU.max
+                )
+            nc.vector.tensor_scalar_mul(out=nb[:], in0=mt[:], scalar1=-SOFTCAP)
+            state[b] = {"tb": tb, "nb": nb}
+
+        def stage_b(b):
+            st = state[b]
+            tb = st["tb"]
+            nb = st["nb"]
+            ls = small.tile([P, TB], F32, tag="ls")
+            grp = gp.tile([P, TB, P, 4], BF16, tag="grp", align_bytes=64)
+            pb = pb0 if b < 2 else pb1
+            for i in range(TB):
+                n = TB * b + i
+                j = n % 8
+                lo = max(0, 8 - n)
+                c0 = 8 * j if b >= 2 else 8 * j - 64
+                nc.scalar.activation(
+                    out=pb[:, j, :, c0 + 8 * lo : c0 + CW].rearrange("p t (g e) -> p g t e", e=8),
+                    in_=tb[:, lo:NG, i, :].rearrange("p g (t e) -> p g t e", e=8),
+                    func=ACT.Exp,
+                    scale=SOFTCAP,
+                    bias=nb[:, i : i + 1],
+                    accum_out=ls[:, i : i + 1],
+                )
+            for k in range(2):
+                tp = ps_t.tile([P, 1024], BF16, tag="tp")
+                for i in range(2):
+                    j = (TB * b + 2 * k + i) % 8
+                    for t in range(4):
+                        m = 4 * i + t
+                        nc.tensor.transpose(tp[:, P * m : P * (m + 1)], pb[:, j, t, :], ident[:])
+                src = tp[:].rearrange("c (i t p) -> c i p t", i=2, t=4)
+                dst = grp[:, 2 * k : 2 * k + 2, :, :]
+                if ACT_COPIES[(2 * b + k) % len(ACT_COPIES)]:
+                    nc.scalar.copy(out=dst, in_=src)
+                else:
+                    nc.vector.tensor_copy(out=dst, in_=src)
+            st["ls"] = ls
+            st["grp"] = grp
+
+        def stage_c(b):
+            st = state[b]
+            pw = gp.tile([P, TB * P], U32, tag="pw", align_bytes=64)
+            psc = gp.tile([P, TB * P], U8, tag="psc", align_bytes=64)
+            rl = small.tile([P, TB], F32, tag="rl")
+            ob = ps_o.tile([P, TB, D], F32, tag="ob")
+            osb = op.tile([P, TB, D], F32, tag="osb")
+            nc.vector.quantize_mx(
+                out=pw[:].bitcast(FP8X4),
+                scales=psc[:],
+                in_=st["grp"][:].rearrange("c i p t -> c (i p t)"),
+            )
+            nc.vector.tensor_scalar_add(out=rl[:], in0=st["ls"][:], scalar1=EPS)
+            nc.vector.reciprocal(out=rl[:], in_=rl[:])
+            v = max(0, b // 2 - 1)
+            for i in range(TB):
+                nc.tensor.matmul_mx(
+                    out=ob[:, i, :],
+                    lhsT=pw[:, P * i : P * (i + 1)].bitcast(FP8X4),
+                    lhsT_scale=psc[:, P * i : P * (i + 1)],
+                    rhs=v_w[:, D * v : D * (v + 1)].bitcast(FP8X4),
+                    rhs_scale=v_s[:, D * v : D * (v + 1)],
+                    start=True,
+                    stop=True,
+                )
+            nc.vector.tensor_tensor(
+                out=osb[:],
+                in0=ob[:],
+                in1=rl[:].unsqueeze(2).to_broadcast([P, TB, D]),
+                op=ALU.mult,
+            )
+            for h in range(H):
+                nc.sync.dma_start(
+                    out=out[0, h, P * b : P * (b + 1), :].rearrange("(i q) d -> q i d", q=QB),
+                    in_=osb[h:P:H, :, :],
+                )
+
+        k_transposes(0)
+        q_transposes(0)
+        for step in range(NB + 2):
+            if step < NB:
+                stage_a(step)
+            if step == 0:
+                k_transposes(2)
+                q_transposes(1)
+                v_prep(0, 4)
+            if step == 1:
+                v_quant(0, 4)
+                v_prep(4, 6)
+                v_prep(6, 7)
+            if step == 2:
+                v_quant(4, 6)
+                v_quant(6, 7)
+            if step % 2 == 1 and (step + 3) // 2 < 8:
+                q_transposes((step + 3) // 2)
+            if 1 <= step <= NB:
+                stage_b(step - 1)
+            if step >= 2:
+                stage_c(step - 2)

@@ -32,20 +32,19 @@ NV = 7
 
 FLOPS = 4 * H * D * (S * (WIN + 1) - WIN * (WIN + 1) // 2)
 
-ACT_COPIES = (1, 0, 1, 1, 0, 1, 0, 1)
-
 
 def tile_modelnew_kernel(tc, Q, K, V, out):
     nc = tc.nc
     with ExitStack() as ctx:
+        ctx.enter_context(tc.manual_schedule())
         const = ctx.enter_context(tc.tile_pool(name="const", bufs=1))
         tbp = ctx.enter_context(tc.tile_pool(name="tbp", bufs=4))
         small = ctx.enter_context(tc.tile_pool(name="small", bufs=6))
         gp = ctx.enter_context(tc.tile_pool(name="gp", bufs=3))
         op = ctx.enter_context(tc.tile_pool(name="op", bufs=4))
-        ps_s = ctx.enter_context(tc.psum_pool(name="ps_s", bufs=3))
+        ps_s = ctx.enter_context(tc.psum_pool(name="ps_s", bufs=4))
         ps_t = ctx.enter_context(tc.psum_pool(name="ps_t", bufs=3))
-        ps_o = ctx.enter_context(tc.psum_pool(name="ps_o", bufs=2))
+        ps_o = ctx.enter_context(tc.psum_pool(name="ps_o", bufs=1))
 
         k_sb = const.tile([P, 4, 4, D], BF16)
         q_sb = const.tile([P, NT, D], BF16)
@@ -90,25 +89,27 @@ def tile_modelnew_kernel(tc, Q, K, V, out):
                 in_=V[0, 0, 256 * v : 256 * v + 512, :].rearrange("(p t) d -> p t d", t=4),
             )
 
-        def k_transposes(g0):
-            tp = ps_t.tile([P, 1024], BF16, tag="tp")
-            for g in range(2):
-                for t in range(4):
-                    n = 4 * g + t
-                    nc.tensor.transpose(tp[:, P * n : P * (n + 1)], k_sb[:, g0 + g, t, :], ident[:])
-            for g in range(2):
-                nc.vector.tensor_copy(
-                    out=kt[:, 16 * (g0 + g) : 16 * (g0 + g + 1), :, :],
-                    in_=tp[:, 512 * g : 512 * (g + 1)].rearrange("d (t l e) -> d l t e", t=4, e=8),
-                )
+        kt_flat = kt[:].rearrange("d l t e -> d (l t e)")
+        state = {}
 
-        def q_transposes(n8):
+        def k_transposes(g):
+            tp = ps_t.tile([P, 1024], BF16, tag="tp")
+            for t in range(4):
+                nc.tensor.transpose(tp[:, P * t : P * (t + 1)], k_sb[:, g, t, :], ident[:])
+            nc.vector.tensor_copy(
+                out=kt[:, 16 * g : 16 * (g + 1), :, :],
+                in_=tp[:, 0:512].rearrange("d (t l e) -> d l t e", t=4, e=8),
+            )
+
+        def q_transposes(n8, on_scalar):
             tp = ps_t.tile([P, 1024], BF16, tag="tp")
             for n in range(8):
                 nc.tensor.transpose(tp[:, P * n : P * (n + 1)], q_sb[:, 8 * n8 + n, :], ident[:])
-            nc.vector.tensor_copy(
-                out=qt[:, 8 * n8 : 8 * (n8 + 1), :].rearrange("d n p -> d (n p)"), in_=tp[:]
-            )
+            dst = qt[:, 8 * n8 : 8 * (n8 + 1), :].rearrange("d n p -> d (n p)")
+            if on_scalar:
+                nc.scalar.copy(out=dst, in_=tp[:])
+            else:
+                nc.vector.tensor_copy(out=dst, in_=tp[:])
 
         def v_prep(v0, v1):
             nc.vector.tensor_copy(
@@ -118,34 +119,40 @@ def tile_modelnew_kernel(tc, Q, K, V, out):
 
         def v_quant(v0, v1):
             nc.vector.quantize_mx(
-                out=v_w[:, D * v0 : D * v1].bitcast(FP8X4),
+                out=v_w[:, D * v0 : D * (v1)].bitcast(FP8X4),
                 scales=v_s[:, D * v0 : D * v1],
                 in_=v_grp[:, v0:v1, :, :].rearrange("p v d t -> p (v d t)"),
             )
 
-        state = {}
-        kt_flat = kt[:].rearrange("d l t e -> d (l t e)")
+        def scores(b, i):
+            n = TB * b + i
+            lo = max(0, 8 - n)
+            sc = ps_s.tile([P, NG, 32], F32, tag="sc")
+            nc.tensor.matmul(
+                out=sc[:, lo:NG, :].rearrange("p g e -> p (g e)"),
+                lhsT=qt[:, n, :],
+                rhs=kt_flat[:, 32 * (n - 8 + lo) : 32 * (n + 1)],
+                start=True,
+                stop=True,
+            )
+            state[("sc", n)] = sc
 
-        def stage_a(b):
-            tb = tbp.tile([P, NG, TB, 32], F32, tag="tb")
-            mt = small.tile([P, TB], F32, tag="mt")
-            nb = small.tile([P, TB], F32, tag="nb")
-            first = b < 2
-            for i in range(TB):
-                n = TB * b + i
-                lo = max(0, 8 - n)
-                sc = ps_s.tile([P, NG, 32], F32, tag="sc")
-                nc.tensor.matmul(
-                    out=sc[:, lo:NG, :].rearrange("p g e -> p (g e)"),
-                    lhsT=qt[:, n, :],
-                    rhs=kt_flat[:, 32 * (n - 8 + lo) : 32 * (n + 1)],
-                    start=True,
-                    stop=True,
-                )
-                nc.scalar.activation(
-                    out=tb[:, lo:NG, i, :], in_=sc[:, lo:NG, :], func=ACT.Tanh, scale=SCALE / SOFTCAP
-                )
-            if not first:
+        def tanh(b, i):
+            n = TB * b + i
+            lo = max(0, 8 - n)
+            if i == 0:
+                tb_new = tbp.tile([P, NG, TB, 32], F32, tag="tb")
+                state[("tb", b)] = tb_new
+            nc.scalar.activation(
+                out=state[("tb", b)][:, lo:NG, i, :],
+                in_=state[("sc", n)][:, lo:NG, :],
+                func=ACT.Tanh,
+                scale=SCALE / SOFTCAP,
+            )
+
+        def masks(b):
+            tb = state[("tb", b)]
+            if b >= 2:
                 nc.gpsimd.affine_select(
                     out=tb[:, 0, :, :].rearrange("p i e -> p (i e)"),
                     in_=tb[:, 0, :, :].rearrange("p i e -> p (i e)"),
@@ -164,7 +171,12 @@ def tile_modelnew_kernel(tc, Q, K, V, out):
                 base=0,
                 channel_multiplier=1,
             )
-            if first:
+
+        def row_max(b):
+            tb = state[("tb", b)]
+            mt = small.tile([P, TB], F32, tag="mt")
+            nb = small.tile([P, TB], F32, tag="nb")
+            if b < 2:
                 for i in range(TB):
                     lo = max(0, 8 - (TB * b + i))
                     nc.vector.tensor_reduce(
@@ -175,58 +187,72 @@ def tile_modelnew_kernel(tc, Q, K, V, out):
                     out=mt[:], in_=tb[:].rearrange("p g i e -> p i g e"), axis=AX.XY, op=ALU.max
                 )
             nc.vector.tensor_scalar_mul(out=nb[:], in0=mt[:], scalar1=-SOFTCAP)
-            state[b] = {"tb": tb, "nb": nb}
+            state[("nb", b)] = nb
 
-        def stage_b(b):
-            st = state[b]
-            tb = st["tb"]
-            nb = st["nb"]
-            ls = small.tile([P, TB], F32, tag="ls")
-            grp = gp.tile([P, TB, P, 4], BF16, tag="grp", align_bytes=64)
+        def exps(b, i):
+            n = TB * b + i
+            j = n % 8
+            lo = max(0, 8 - n)
+            c0 = 8 * j if b >= 2 else 8 * j - 64
             pb = pb0 if b < 2 else pb1
-            for i in range(TB):
-                n = TB * b + i
-                j = n % 8
-                lo = max(0, 8 - n)
-                c0 = 8 * j if b >= 2 else 8 * j - 64
-                nc.scalar.activation(
-                    out=pb[:, j, :, c0 + 8 * lo : c0 + CW].rearrange("p t (g e) -> p g t e", e=8),
-                    in_=tb[:, lo:NG, i, :].rearrange("p g (t e) -> p g t e", e=8),
-                    func=ACT.Exp,
-                    scale=SOFTCAP,
-                    bias=nb[:, i : i + 1],
-                    accum_out=ls[:, i : i + 1],
-                )
-            for k in range(2):
-                tp = ps_t.tile([P, 1024], BF16, tag="tp")
-                for i in range(2):
-                    j = (TB * b + 2 * k + i) % 8
-                    for t in range(4):
-                        m = 4 * i + t
-                        nc.tensor.transpose(tp[:, P * m : P * (m + 1)], pb[:, j, t, :], ident[:])
-                src = tp[:].rearrange("c (i t p) -> c i p t", i=2, t=4)
-                dst = grp[:, 2 * k : 2 * k + 2, :, :]
-                if ACT_COPIES[(2 * b + k) % len(ACT_COPIES)]:
-                    nc.scalar.copy(out=dst, in_=src)
-                else:
-                    nc.vector.tensor_copy(out=dst, in_=src)
-            st["ls"] = ls
-            st["grp"] = grp
+            if i == 0:
+                ls_new = small.tile([P, TB], F32, tag="ls")
+                state[("ls", b)] = ls_new
+            nc.scalar.activation(
+                out=pb[:, j, :, c0 + 8 * lo : c0 + CW].rearrange("p t (g e) -> p g t e", e=8),
+                in_=state[("tb", b)][:, lo:NG, i, :].rearrange("p g (t e) -> p g t e", e=8),
+                func=ACT.Exp,
+                scale=SOFTCAP,
+                bias=state[("nb", b)][:, i : i + 1],
+                accum_out=state[("ls", b)][:, i : i + 1],
+            )
 
-        def stage_c(b):
-            st = state[b]
+        def p_transposes(b, k):
+            pb = pb0 if b < 2 else pb1
+            tp = ps_t.tile([P, 1024], BF16, tag="tp")
+            for i in range(2):
+                j = (TB * b + 2 * k + i) % 8
+                for t in range(4):
+                    m = 4 * i + t
+                    if i == 0:
+                        nc.tensor.matmul(
+                            out=tp[:, P * m : P * (m + 1)],
+                            lhsT=pb[:, j, t, :],
+                            rhs=ident[:],
+                            start=True,
+                            stop=True,
+                        )
+                    else:
+                        nc.tensor.transpose(tp[:, P * m : P * (m + 1)], pb[:, j, t, :], ident[:])
+            state[("tp", b, k)] = tp
+
+        def copy_out(b, k, on_scalar):
+            if ("grp", b) not in state:
+                grp_new = gp.tile([P, TB, P, 4], BF16, tag="grp", align_bytes=64)
+                state[("grp", b)] = grp_new
+            src = state[("tp", b, k)][:].rearrange("c (i t p) -> c i p t", i=2, t=4)
+            dst = state[("grp", b)][:, 2 * k : 2 * k + 2, :, :]
+            if on_scalar:
+                nc.scalar.copy(out=dst, in_=src)
+            else:
+                nc.vector.tensor_copy(out=dst, in_=src)
+
+        def quantise(b):
             pw = gp.tile([P, TB * P], U32, tag="pw", align_bytes=64)
             psc = gp.tile([P, TB * P], U8, tag="psc", align_bytes=64)
             rl = small.tile([P, TB], F32, tag="rl")
-            ob = ps_o.tile([P, TB, D], F32, tag="ob")
-            osb = op.tile([P, TB, D], F32, tag="osb")
             nc.vector.quantize_mx(
                 out=pw[:].bitcast(FP8X4),
                 scales=psc[:],
-                in_=st["grp"][:].rearrange("c i p t -> c (i p t)"),
+                in_=state[("grp", b)][:].rearrange("c i p t -> c (i p t)"),
             )
-            nc.vector.tensor_scalar_add(out=rl[:], in0=st["ls"][:], scalar1=EPS)
+            nc.vector.tensor_scalar_add(out=rl[:], in0=state[("ls", b)][:], scalar1=EPS)
             nc.vector.reciprocal(out=rl[:], in_=rl[:])
+            state[("pw", b)] = (pw, psc, rl)
+
+        def mx(b):
+            pw, psc, rl = state[("pw", b)]
+            ob = ps_o.tile([P, TB, D], F32, tag="ob")
             v = max(0, b // 2 - 1)
             for i in range(TB):
                 nc.tensor.matmul_mx(
@@ -238,9 +264,14 @@ def tile_modelnew_kernel(tc, Q, K, V, out):
                     start=True,
                     stop=True,
                 )
+            state[("ob", b)] = ob
+
+        def finish(b):
+            rl = state[("pw", b)][2]
+            osb = op.tile([P, TB, D], F32, tag="osb")
             nc.vector.tensor_tensor(
                 out=osb[:],
-                in0=ob[:],
+                in0=state[("ob", b)][:],
                 in1=rl[:].unsqueeze(2).to_broadcast([P, TB, D]),
                 op=ALU.mult,
             )
@@ -251,24 +282,47 @@ def tile_modelnew_kernel(tc, Q, K, V, out):
                 )
 
         k_transposes(0)
-        q_transposes(0)
-        for step in range(NB + 2):
-            if step < NB:
-                stage_a(step)
-            if step == 0:
-                k_transposes(2)
-                q_transposes(1)
+        q_transposes(0, True)
+        for i in range(TB):
+            scores(0, i)
+        for s in range(NB + 4):
+            if s < NB:
+                for i in range(TB):
+                    tanh(s, i)
+                masks(s)
+            if 2 <= s < NB + 2:
+                p_transposes(s - 2, 1)
+            if 3 <= s < NB + 3:
+                mx(s - 3)
+            if s + 1 < NB:
+                for i in range(TB):
+                    scores(s + 1, i)
+            if 1 <= s < NB + 1:
+                row_max(s - 1)
+            if 3 <= s < NB + 3:
+                finish(s - 3)
+            if 2 <= s < NB + 2:
+                copy_out(s - 2, 1, True)
+                copy_out(s - 2, 0, False)
+                quantise(s - 2)
+            if s == 0:
+                q_transposes(1, False)
                 v_prep(0, 4)
-            if step == 1:
+            if s == 1:
+                k_transposes(1)
                 v_quant(0, 4)
                 v_prep(4, 6)
                 v_prep(6, 7)
-            if step == 2:
+            if s == 2:
+                k_transposes(2)
+                k_transposes(3)
                 v_quant(4, 6)
                 v_quant(6, 7)
-            if step % 2 == 1 and (step + 3) // 2 < 8:
-                q_transposes((step + 3) // 2)
-            if 1 <= step <= NB:
-                stage_b(step - 1)
-            if step >= 2:
-                stage_c(step - 2)
+            if s % 2 == 1 and (s + 3) // 2 < 8:
+                q_transposes((s + 3) // 2, False)
+            if 1 <= s < NB + 1:
+                exps(s - 1, 0)
+                exps(s - 1, 1)
+                p_transposes(s - 1, 0)
+                exps(s - 1, 2)
+                exps(s - 1, 3)

@@ -214,7 +214,7 @@ def tile_modelnew_kernel(tc, Q, K, V, out):
                 j = (TB * b + 2 * k + i) % 8
                 for t in range(4):
                     m = 4 * i + t
-                    if i == 0:
+                    if m < 5:
                         nc.tensor.matmul(
                             out=tp[:, P * m : P * (m + 1)],
                             lhsT=pb[:, j, t, :],
@@ -295,8 +295,8 @@ def tile_modelnew_kernel(tc, Q, K, V, out):
             if 3 <= s < NB + 3:
                 mx(s - 3)
             if s + 1 < NB:
-                for i in range(TB):
-                    scores(s + 1, i)
+                scores(s + 1, 0)
+                scores(s + 1, 1)
             if 1 <= s < NB + 1:
                 row_max(s - 1)
             if 3 <= s < NB + 3:
@@ -324,5 +324,9 @@ def tile_modelnew_kernel(tc, Q, K, V, out):
                 exps(s - 1, 0)
                 exps(s - 1, 1)
                 p_transposes(s - 1, 0)
+            if s + 1 < NB:
+                scores(s + 1, 2)
+                scores(s + 1, 3)
+            if 1 <= s < NB + 1:
                 exps(s - 1, 2)
                 exps(s - 1, 3)

@@ -42,8 +42,8 @@ def tile_modelnew_kernel(tc, Q, K, V, out):
         small = ctx.enter_context(tc.tile_pool(name="small", bufs=6))
         gp = ctx.enter_context(tc.tile_pool(name="gp", bufs=3))
         op = ctx.enter_context(tc.tile_pool(name="op", bufs=4))
-        ps_s = ctx.enter_context(tc.psum_pool(name="ps_s", bufs=4))
-        ps_t = ctx.enter_context(tc.psum_pool(name="ps_t", bufs=3))
+        ps_s = ctx.enter_context(tc.psum_pool(name="ps_s", bufs=3))
+        ps_t = ctx.enter_context(tc.psum_pool(name="ps_t", bufs=4))
         ps_o = ctx.enter_context(tc.psum_pool(name="ps_o", bufs=1))
 
         k_sb = const.tile([P, 4, 4, D], BF16)
@@ -75,19 +75,24 @@ def tile_modelnew_kernel(tc, Q, K, V, out):
                     in_=Q[0, h, QB * t0 : QB * t1, :].rearrange("(n q) d -> q n d", q=QB),
                 )
 
+        def load_v(v):
+            nc.sync.dma_start(
+                out=v_raw[:, v, :, :],
+                in_=V[0, 0, 256 * v : 256 * v + 512, :].rearrange("(p t) d -> p t d", t=4),
+            )
+
         load_k(0)
         load_q(0, 8)
         load_k(1)
         load_q(8, 16)
+        for v in range(4):
+            load_v(v)
         load_k(2)
         load_k(3)
         load_q(16, 32)
+        for v in range(4, NV):
+            load_v(v)
         load_q(32, 64)
-        for v in range(NV):
-            nc.scalar.dma_start(
-                out=v_raw[:, v, :, :],
-                in_=V[0, 0, 256 * v : 256 * v + 512, :].rearrange("(p t) d -> p t d", t=4),
-            )
 
         kt_flat = kt[:].rearrange("d l t e -> d (l t e)")
         state = {}
@@ -124,8 +129,7 @@ def tile_modelnew_kernel(tc, Q, K, V, out):
                 in_=v_grp[:, v0:v1, :, :].rearrange("p v d t -> p (v d t)"),
             )
 
-        def scores(b, i):
-            n = TB * b + i
+        def scores(n):
             lo = max(0, 8 - n)
             sc = ps_s.tile([P, NG, 32], F32, tag="sc")
             nc.tensor.matmul(
@@ -186,8 +190,13 @@ def tile_modelnew_kernel(tc, Q, K, V, out):
                 nc.vector.tensor_reduce(
                     out=mt[:], in_=tb[:].rearrange("p g i e -> p i g e"), axis=AX.XY, op=ALU.max
                 )
-            nc.vector.tensor_scalar_mul(out=nb[:], in0=mt[:], scalar1=-SOFTCAP)
+            state[("mt", b)] = mt
             state[("nb", b)] = nb
+
+        def neg_bias(b):
+            nc.gpsimd.tensor_scalar(
+                out=state[("nb", b)][:], in0=state[("mt", b)][:], scalar1=-SOFTCAP, scalar2=0.0, op0=ALU.mult, op1=ALU.add
+            )
 
         def exps(b, i):
             n = TB * b + i
@@ -240,18 +249,27 @@ def tile_modelnew_kernel(tc, Q, K, V, out):
         def quantise(b):
             pw = gp.tile([P, TB * P], U32, tag="pw", align_bytes=64)
             psc = gp.tile([P, TB * P], U8, tag="psc", align_bytes=64)
-            rl = small.tile([P, TB], F32, tag="rl")
             nc.vector.quantize_mx(
                 out=pw[:].bitcast(FP8X4),
                 scales=psc[:],
                 in_=state[("grp", b)][:].rearrange("c i p t -> c (i p t)"),
             )
-            nc.vector.tensor_scalar_add(out=rl[:], in0=state[("ls", b)][:], scalar1=EPS)
-            nc.vector.reciprocal(out=rl[:], in_=rl[:])
-            state[("pw", b)] = (pw, psc, rl)
+            state[("pw", b)] = (pw, psc)
+
+        def l_eps(b):
+            le = small.tile([P, TB], F32, tag="le")
+            nc.gpsimd.tensor_scalar(
+                out=le[:], in0=state[("ls", b)][:], scalar1=1.0, scalar2=EPS, op0=ALU.mult, op1=ALU.add
+            )
+            state[("le", b)] = le
+
+        def recip(b):
+            rl = small.tile([P, TB], F32, tag="rl")
+            nc.vector.reciprocal(out=rl[:], in_=state[("le", b)][:])
+            state[("rl", b)] = rl
 
         def mx(b):
-            pw, psc, rl = state[("pw", b)]
+            pw, psc = state[("pw", b)]
             ob = ps_o.tile([P, TB, D], F32, tag="ob")
             v = max(0, b // 2 - 1)
             for i in range(TB):
@@ -267,7 +285,7 @@ def tile_modelnew_kernel(tc, Q, K, V, out):
             state[("ob", b)] = ob
 
         def finish(b):
-            rl = state[("pw", b)][2]
+            rl = state[("rl", b)]
             osb = op.tile([P, TB, D], F32, tag="osb")
             nc.vector.tensor_tensor(
                 out=osb[:],
@@ -283,50 +301,51 @@ def tile_modelnew_kernel(tc, Q, K, V, out):
 
         k_transposes(0)
         q_transposes(0, True)
-        for i in range(TB):
-            scores(0, i)
-        for s in range(NB + 4):
-            if s < NB:
-                for i in range(TB):
-                    tanh(s, i)
-                masks(s)
-            if 2 <= s < NB + 2:
-                p_transposes(s - 2, 1)
-            if 3 <= s < NB + 3:
-                mx(s - 3)
-            if s + 1 < NB:
-                scores(s + 1, 0)
-                scores(s + 1, 1)
+        for n in range(3):
+            scores(n)
+        for s in range(NB + 5):
             if 1 <= s < NB + 1:
                 row_max(s - 1)
-            if 3 <= s < NB + 3:
-                finish(s - 3)
+                neg_bias(s - 1)
+            for i in range(TB):
+                if s < NB:
+                    tanh(s, i)
+                    if TB * s + i + 3 < NT:
+                        scores(TB * s + i + 3)
+                if i == 2 and 4 <= s < NB + 4:
+                    mx(s - 4)
+                if i == 2 and 3 <= s < NB + 3:
+                    copy_out(s - 3, 1, False)
+                if 2 <= s < NB + 2:
+                    exps(s - 2, i)
+                    if i == 1:
+                        p_transposes(s - 2, 0)
+                    if i == 3:
+                        p_transposes(s - 2, 1)
+            if s < NB:
+                masks(s)
             if 2 <= s < NB + 2:
-                copy_out(s - 2, 1, True)
-                copy_out(s - 2, 0, False)
-                quantise(s - 2)
+                l_eps(s - 2)
+                copy_out(s - 2, 0, True)
+            if 4 <= s < NB + 4:
+                finish(s - 4)
+            if 3 <= s < NB + 3:
+                quantise(s - 3)
+                recip(s - 3)
             if s == 0:
                 q_transposes(1, False)
-                v_prep(0, 4)
-            if s == 1:
                 k_transposes(1)
+            if s == 1:
+                k_transposes(2)
+                k_transposes(3)
+            if s == 2:
+                v_prep(0, 4)
+            if s == 3:
                 v_quant(0, 4)
                 v_prep(4, 6)
                 v_prep(6, 7)
-            if s == 2:
-                k_transposes(2)
-                k_transposes(3)
+            if s == 4:
                 v_quant(4, 6)
                 v_quant(6, 7)
             if s % 2 == 1 and (s + 3) // 2 < 8:
                 q_transposes((s + 3) // 2, False)
-            if 1 <= s < NB + 1:
-                exps(s - 1, 0)
-                exps(s - 1, 1)
-                p_transposes(s - 1, 0)
-            if s + 1 < NB:
-                scores(s + 1, 2)
-                scores(s + 1, 3)
-            if 1 <= s < NB + 1:
-                exps(s - 1, 2)
-                exps(s - 1, 3)

@@ -58,14 +58,13 @@ def tile_modelnew_kernel(tc, Q, K, V, out):
         pb1 = const.tile([P, 8, 4, P], BF16)
         ident = const.tile([P, P], BF16)
 
-        nc.vector.memset(pb0[:].bitcast(I32), 0)
-        nc.vector.memset(pb1[:].bitcast(I32), 0)
         make_identity(nc, ident[:])
+        nc.vector.memset(pb0[:].bitcast(I32), 0)
 
-        def load_k(g):
+        def load_k(g0, g1):
             nc.sync.dma_start(
-                out=k_sb[:, g, :, :],
-                in_=K[0, 0, 512 * g : 512 * (g + 1), :].rearrange("(c t) d -> c t d", t=4),
+                out=k_sb[:, g0:g1, :, :].rearrange("c g t d -> c g (t d)"),
+                in_=K[0, 0, 512 * g0 : 512 * g1, :].rearrange("(g c t) d -> c g (t d)", c=P, t=4),
             )
 
         def load_q(t0, t1):
@@ -75,46 +74,50 @@ def tile_modelnew_kernel(tc, Q, K, V, out):
                     in_=Q[0, h, QB * t0 : QB * t1, :].rearrange("(n q) d -> q n d", q=QB),
                 )
 
-        def load_v(v):
+        def load_v(first, count):
             nc.sync.dma_start(
-                out=v_raw[:, v, :, :],
-                in_=V[0, 0, 256 * v : 256 * v + 512, :].rearrange("(p t) d -> p t d", t=4),
+                out=v_raw[:, first:NV:2, :, :].rearrange("p v t d -> p v (t d)"),
+                in_=V[0, 0, 256 * first : 256 * first + 512 * count, :].rearrange("(v p t) d -> p v (t d)", p=P, t=4),
             )
 
-        load_k(0)
-        load_q(0, 8)
-        load_k(1)
-        load_q(8, 16)
-        for v in range(4):
-            load_v(v)
-        load_k(2)
-        load_k(3)
+        load_k(0, 1)
+        load_q(0, 4)
+        load_q(4, 16)
+        load_k(1, 4)
         load_q(16, 32)
-        for v in range(4, NV):
-            load_v(v)
+        load_v(0, 4)
+        load_v(1, 3)
         load_q(32, 64)
 
         kt_flat = kt[:].rearrange("d l t e -> d (l t e)")
         state = {}
 
-        def k_transposes(g):
+        def k_tr(g):
             tp = ps_t.tile([P, 1024], BF16, tag="tp")
             for t in range(4):
                 nc.tensor.transpose(tp[:, P * t : P * (t + 1)], k_sb[:, g, t, :], ident[:])
+            state[("ktp", g)] = tp
+
+        def k_copy(g):
+            tp = state[("ktp", g)]
             nc.vector.tensor_copy(
                 out=kt[:, 16 * g : 16 * (g + 1), :, :],
                 in_=tp[:, 0:512].rearrange("d (t l e) -> d l t e", t=4, e=8),
             )
 
-        def q_transposes(n8, on_scalar):
+        def q_tr(n0, n1):
             tp = ps_t.tile([P, 1024], BF16, tag="tp")
-            for n in range(8):
-                nc.tensor.transpose(tp[:, P * n : P * (n + 1)], q_sb[:, 8 * n8 + n, :], ident[:])
-            dst = qt[:, 8 * n8 : 8 * (n8 + 1), :].rearrange("d n p -> d (n p)")
+            for n in range(n0, n1):
+                nc.tensor.transpose(tp[:, P * (n - n0) : P * (n - n0 + 1)], q_sb[:, n, :], ident[:])
+            state[("qtp", n0)] = tp
+
+        def q_copy(n0, n1, on_scalar):
+            dst = qt[:, n0:n1, :].rearrange("d n p -> d (n p)")
+            src = state[("qtp", n0)][:, 0 : P * (n1 - n0)]
             if on_scalar:
-                nc.scalar.copy(out=dst, in_=tp[:])
+                nc.scalar.copy(out=dst, in_=src)
             else:
-                nc.vector.tensor_copy(out=dst, in_=tp[:])
+                nc.vector.tensor_copy(out=dst, in_=src)
 
         def v_prep(v0, v1):
             nc.vector.tensor_copy(
@@ -131,7 +134,8 @@ def tile_modelnew_kernel(tc, Q, K, V, out):
 
         def scores(n):
             lo = max(0, 8 - n)
-            sc = ps_s.tile([P, NG, 32], F32, tag="sc")
+            bank = ps_s.tile([P, TB * D], F32, tag="sc")
+            sc = bank[:, 0 : 32 * NG].rearrange("p (g e) -> p g e", e=32)
             nc.tensor.matmul(
                 out=sc[:, lo:NG, :].rearrange("p g e -> p (g e)"),
                 lhsT=qt[:, n, :],
@@ -246,15 +250,17 @@ def tile_modelnew_kernel(tc, Q, K, V, out):
             else:
                 nc.vector.tensor_copy(out=dst, in_=src)
 
-        def quantise(b):
-            pw = gp.tile([P, TB * P], U32, tag="pw", align_bytes=64)
-            psc = gp.tile([P, TB * P], U8, tag="psc", align_bytes=64)
+        def quantise(b, i0, i1):
+            if ("pw", b) not in state:
+                pw_new = gp.tile([P, TB * P], U32, tag="pw", align_bytes=64)
+                psc_new = gp.tile([P, TB * P], U8, tag="psc", align_bytes=64)
+                state[("pw", b)] = (pw_new, psc_new)
+            pw, psc = state[("pw", b)]
             nc.vector.quantize_mx(
-                out=pw[:].bitcast(FP8X4),
-                scales=psc[:],
-                in_=state[("grp", b)][:].rearrange("c i p t -> c (i p t)"),
+                out=pw[:, P * i0 : P * i1].bitcast(FP8X4),
+                scales=psc[:, P * i0 : P * i1],
+                in_=state[("grp", b)][:, i0:i1, :, :].rearrange("c i p t -> c (i p t)"),
             )
-            state[("pw", b)] = (pw, psc)
 
         def l_eps(b):
             le = small.tile([P, TB], F32, tag="le")
@@ -268,13 +274,16 @@ def tile_modelnew_kernel(tc, Q, K, V, out):
             nc.vector.reciprocal(out=rl[:], in_=state[("le", b)][:])
             state[("rl", b)] = rl
 
-        def mx(b):
+        def mx(b, i0, i1, spare):
             pw, psc = state[("pw", b)]
-            ob = ps_o.tile([P, TB, D], F32, tag="ob")
+            if spare:
+                ob = ps_s.tile([P, TB * D], F32, tag="sc")
+            else:
+                ob = ps_o.tile([P, TB * D], F32, tag="ob")
             v = max(0, b // 2 - 1)
-            for i in range(TB):
+            for i in range(i0, i1):
                 nc.tensor.matmul_mx(
-                    out=ob[:, i, :],
+                    out=ob[:, D * i : D * (i + 1)],
                     lhsT=pw[:, P * i : P * (i + 1)].bitcast(FP8X4),
                     lhsT_scale=psc[:, P * i : P * (i + 1)],
                     rhs=v_w[:, D * v : D * (v + 1)].bitcast(FP8X4),
@@ -282,62 +291,75 @@ def tile_modelnew_kernel(tc, Q, K, V, out):
                     start=True,
                     stop=True,
                 )
-            state[("ob", b)] = ob
+            state[("ob", b, i0)] = ob
 
-        def finish(b):
+        def finish(b, i0, i1, on_scalar):
             rl = state[("rl", b)]
+            ob = state[("ob", b, i0)]
             osb = op.tile([P, TB, D], F32, tag="osb")
-            nc.vector.tensor_tensor(
-                out=osb[:],
-                in0=state[("ob", b)][:],
-                in1=rl[:].unsqueeze(2).to_broadcast([P, TB, D]),
-                op=ALU.mult,
-            )
+            if on_scalar:
+                for i in range(i0, i1):
+                    nc.scalar.activation(out=osb[:, i, :], in_=ob[:, D * i : D * (i + 1)], func=ACT.Copy, scale=rl[:, i : i + 1])
+            else:
+                nc.vector.tensor_tensor(
+                    out=osb[:, i0:i1, :],
+                    in0=ob[:, D * i0 : D * i1].rearrange("p (i d) -> p i d", d=D),
+                    in1=rl[:, i0:i1].unsqueeze(2).to_broadcast([P, i1 - i0, D]),
+                    op=ALU.mult,
+                )
             for h in range(H):
                 nc.sync.dma_start(
-                    out=out[0, h, P * b : P * (b + 1), :].rearrange("(i q) d -> q i d", q=QB),
-                    in_=osb[h:P:H, :, :],
+                    out=out[0, h, P * b + QB * i0 : P * b + QB * i1, :].rearrange("(i q) d -> q i d", q=QB),
+                    in_=osb[h:P:H, i0:i1, :],
                 )
 
-        k_transposes(0)
-        q_transposes(0, True)
+        k_tr(0)
+        q_tr(0, 4)
+        k_copy(0)
+        q_copy(0, 4, True)
         for n in range(3):
             scores(n)
-        for s in range(NB + 5):
-            if 1 <= s < NB + 1:
+        q_tr(4, 8)
+        q_copy(4, 8, False)
+        q_tr(8, 16)
+        nc.vector.memset(pb1[:].bitcast(I32), 0)
+        q_copy(8, 16, False)
+        for s in range(NB):
+            q_due = 8 * (s // 2 + 1) if (s % 2 == 0 and 2 <= s <= 12) else 0
+            if 1 <= s:
                 row_max(s - 1)
                 neg_bias(s - 1)
             for i in range(TB):
-                if s < NB:
-                    tanh(s, i)
-                    if TB * s + i + 3 < NT:
-                        scores(TB * s + i + 3)
-                if i == 2 and 4 <= s < NB + 4:
-                    mx(s - 4)
-                if i == 2 and 3 <= s < NB + 3:
+                tanh(s, i)
+                if TB * s + i + 3 < NT:
+                    scores(TB * s + i + 3)
+                if i == 0 and q_due:
+                    q_tr(q_due, q_due + 8)
+                if i == 0 and 1 <= s < 4:
+                    k_tr(s)
+                if i == 2 and 4 <= s:
+                    mx(s - 4, 0, TB, False)
+                if i == 2 and 3 <= s:
                     copy_out(s - 3, 1, False)
-                if 2 <= s < NB + 2:
+                if 2 <= s:
                     exps(s - 2, i)
                     if i == 1:
                         p_transposes(s - 2, 0)
                     if i == 3:
                         p_transposes(s - 2, 1)
-            if s < NB:
-                masks(s)
-            if 2 <= s < NB + 2:
+            masks(s)
+            if 2 <= s:
                 l_eps(s - 2)
                 copy_out(s - 2, 0, True)
-            if 4 <= s < NB + 4:
-                finish(s - 4)
-            if 3 <= s < NB + 3:
-                quantise(s - 3)
+            if q_due:
+                q_copy(q_due, q_due + 8, False)
+            if 1 <= s < 4:
+                k_copy(s)
+            if 4 <= s:
+                finish(s - 4, 0, TB, False)
+            if 3 <= s:
+                quantise(s - 3, 0, TB)
                 recip(s - 3)
-            if s == 0:
-                q_transposes(1, False)
-                k_transposes(1)
-            if s == 1:
-                k_transposes(2)
-                k_transposes(3)
             if s == 2:
                 v_prep(0, 4)
             if s == 3:
@@ -347,5 +369,34 @@ def tile_modelnew_kernel(tc, Q, K, V, out):
             if s == 4:
                 v_quant(4, 6)
                 v_quant(6, 7)
-            if s % 2 == 1 and (s + 3) // 2 < 8:
-                q_transposes((s + 3) // 2, False)
+        row_max(NB - 1)
+        neg_bias(NB - 1)
+        mx(NB - 4, 0, TB, False)
+        for i in range(TB):
+            exps(NB - 2, i)
+            if i % 2 == 1:
+                p_transposes(NB - 2, i // 2)
+        l_eps(NB - 2)
+        copy_out(NB - 3, 1, False)
+        finish(NB - 4, 0, TB, False)
+        quantise(NB - 3, 0, TB)
+        recip(NB - 3)
+        for i in range(TB):
+            exps(NB - 1, i)
+            if i % 2 == 1:
+                p_transposes(NB - 1, i // 2)
+        l_eps(NB - 1)
+        mx(NB - 3, 0, TB, True)
+        copy_out(NB - 2, 0, True)
+        copy_out(NB - 2, 1, False)
+        copy_out(NB - 1, 0, True)
+        copy_out(NB - 1, 1, False)
+        finish(NB - 3, 0, TB, True)
+        quantise(NB - 2, 0, TB)
+        recip(NB - 2)
+        mx(NB - 2, 0, TB, True)
+        quantise(NB - 1, 0, TB)
+        recip(NB - 1)
+        mx(NB - 1, 0, TB, False)
+        finish(NB - 2, 0, TB, True)
+        finish(NB - 1, 0, TB, False)

@@ -57,9 +57,11 @@ def tile_modelnew_kernel(tc, Q, K, V, out):
         pb0 = const.tile([P, 8, 4, P], BF16)
         pb1 = const.tile([P, 8, 4, P], BF16)
         ident = const.tile([P, P], BF16)
+        eps_t = const.tile([P, 1], F32)
 
         make_identity(nc, ident[:])
         nc.vector.memset(pb0[:].bitcast(I32), 0)
+        nc.vector.memset(eps_t[:], EPS)
 
         def load_k(g0, g1):
             nc.sync.dma_start(
@@ -198,9 +200,7 @@ def tile_modelnew_kernel(tc, Q, K, V, out):
             state[("nb", b)] = nb
 
         def neg_bias(b):
-            nc.gpsimd.tensor_scalar(
-                out=state[("nb", b)][:], in0=state[("mt", b)][:], scalar1=-SOFTCAP, scalar2=0.0, op0=ALU.mult, op1=ALU.add
-            )
+            nc.scalar.mul(state[("nb", b)][:], state[("mt", b)][:], -SOFTCAP)
 
         def exps(b, i):
             n = TB * b + i
@@ -239,6 +239,27 @@ def tile_modelnew_kernel(tc, Q, K, V, out):
                         nc.tensor.transpose(tp[:, P * m : P * (m + 1)], pb[:, j, t, :], ident[:])
             state[("tp", b, k)] = tp
 
+        def stage_out(b, k, on_scalar):
+            stg = gp.tile([P, 1024], BF16, tag="stg")
+            if on_scalar:
+                nc.scalar.copy(out=stg[:], in_=state[("tp", b, k)][:])
+            else:
+                nc.vector.tensor_copy(out=stg[:], in_=state[("tp", b, k)][:])
+            state[("stg", b, k)] = stg
+
+        def regroup(b, k):
+            if ("grp", b) not in state:
+                grp_new = gp.tile([P, TB, P, 4], BF16, tag="grp", align_bytes=64)
+                state[("grp", b)] = grp_new
+            nc.gpsimd.tensor_scalar(
+                out=state[("grp", b)][:, 2 * k : 2 * k + 2, :, :],
+                in0=state[("stg", b, k)][:].rearrange("c (i t p) -> c i p t", i=2, t=4),
+                scalar1=1.0,
+                scalar2=0.0,
+                op0=ALU.mult,
+                op1=ALU.add,
+            )
+
         def copy_out(b, k, on_scalar):
             if ("grp", b) not in state:
                 grp_new = gp.tile([P, TB, P, 4], BF16, tag="grp", align_bytes=64)
@@ -264,9 +285,7 @@ def tile_modelnew_kernel(tc, Q, K, V, out):
 
         def l_eps(b):
             le = small.tile([P, TB], F32, tag="le")
-            nc.gpsimd.tensor_scalar(
-                out=le[:], in0=state[("ls", b)][:], scalar1=1.0, scalar2=EPS, op0=ALU.mult, op1=ALU.add
-            )
+            nc.scalar.activation(out=le[:], in_=state[("ls", b)][:], func=ACT.Identity, bias=eps_t[:, 0:1], scale=1.0)
             state[("le", b)] = le
 
         def recip(b):
@@ -326,9 +345,13 @@ def tile_modelnew_kernel(tc, Q, K, V, out):
         q_copy(8, 16, False)
         for s in range(NB):
             q_due = 8 * (s // 2 + 1) if (s % 2 == 0 and 2 <= s <= 12) else 0
+            if 3 <= s:
+                regroup(s - 3, 0)
+
+            if 2 <= s:
+                neg_bias(s - 2)
             if 1 <= s:
                 row_max(s - 1)
-                neg_bias(s - 1)
             for i in range(TB):
                 tanh(s, i)
                 if TB * s + i + 3 < NT:
@@ -349,10 +372,10 @@ def tile_modelnew_kernel(tc, Q, K, V, out):
                         p_transposes(s - 2, 1)
             masks(s)
             if 2 <= s:
+                stage_out(s - 2, 0, True)
                 l_eps(s - 2)
-                copy_out(s - 2, 0, True)
             if q_due:
-                q_copy(q_due, q_due + 8, False)
+                q_copy(q_due, q_due + 8, True)
             if 1 <= s < 4:
                 k_copy(s)
             if 4 <= s:
@@ -369,8 +392,9 @@ def tile_modelnew_kernel(tc, Q, K, V, out):
             if s == 4:
                 v_quant(4, 6)
                 v_quant(6, 7)
+        regroup(NB - 3, 0)
+        neg_bias(NB - 2)
         row_max(NB - 1)
-        neg_bias(NB - 1)
         mx(NB - 4, 0, TB, False)
         for i in range(TB):
             exps(NB - 2, i)
@@ -381,6 +405,7 @@ def tile_modelnew_kernel(tc, Q, K, V, out):
         finish(NB - 4, 0, TB, False)
         quantise(NB - 3, 0, TB)
         recip(NB - 3)
+        neg_bias(NB - 1)
         for i in range(TB):
             exps(NB - 1, i)
             if i % 2 == 1:

@@ -76,19 +76,21 @@ def tile_modelnew_kernel(tc, Q, K, V, out):
                     in_=Q[0, h, QB * t0 : QB * t1, :].rearrange("(n q) d -> q n d", q=QB),
                 )
 
-        def load_v(first, count):
+        def load_v(first, step, count):
             nc.sync.dma_start(
-                out=v_raw[:, first:NV:2, :, :].rearrange("p v t d -> p v (t d)"),
-                in_=V[0, 0, 256 * first : 256 * first + 512 * count, :].rearrange("(v p t) d -> p v (t d)", p=P, t=4),
+                out=v_raw[:, first : min(NV, first + step * count) : step, :, :].rearrange("p v t d -> p v (t d)"),
+                in_=V[0, 0, 256 * first : 256 * first + 256 * step * count, :].rearrange("(v p t) d -> p v (t d)", p=P, t=4),
             )
 
         load_k(0, 1)
         load_q(0, 4)
         load_q(4, 16)
-        load_k(1, 4)
-        load_q(16, 32)
-        load_v(0, 4)
-        load_v(1, 3)
+        load_k(1, 2)
+        load_q(16, 24)
+        load_v(0, 2, 4)
+        load_v(1, 2, 3)
+        load_q(24, 32)
+        load_k(2, 4)
         load_q(32, 64)
 
         kt_flat = kt[:].rearrange("d l t e -> d (l t e)")
@@ -336,13 +338,9 @@ def tile_modelnew_kernel(tc, Q, K, V, out):
         q_tr(0, 4)
         k_copy(0)
         q_copy(0, 4, True)
+        nc.vector.memset(pb1[:].bitcast(I32), 0)
         for n in range(3):
             scores(n)
-        q_tr(4, 8)
-        q_copy(4, 8, False)
-        q_tr(8, 16)
-        nc.vector.memset(pb1[:].bitcast(I32), 0)
-        q_copy(8, 16, False)
         for s in range(NB):
             q_due = 8 * (s // 2 + 1) if (s % 2 == 0 and 2 <= s <= 12) else 0
             if 3 <= s:
@@ -352,14 +350,21 @@ def tile_modelnew_kernel(tc, Q, K, V, out):
                 neg_bias(s - 2)
             if 1 <= s:
                 row_max(s - 1)
+            if s == 1:
+                q_copy(8, 16, False)
             for i in range(TB):
                 tanh(s, i)
                 if TB * s + i + 3 < NT:
                     scores(TB * s + i + 3)
+                if s == 0 and i == 0:
+                    q_tr(4, 8)
+                    q_copy(4, 8, False)
+                if s == 0 and i == 0:
+                    q_tr(8, 16)
                 if i == 0 and q_due:
                     q_tr(q_due, q_due + 8)
-                if i == 0 and 1 <= s < 4:
-                    k_tr(s)
+                if i == 0 and s in (1, 4, 8):
+                    k_tr((s + 4) // 4)
                 if i == 2 and 4 <= s:
                     mx(s - 4, 0, TB, False)
                 if i == 2 and 3 <= s:
@@ -376,8 +381,8 @@ def tile_modelnew_kernel(tc, Q, K, V, out):
                 l_eps(s - 2)
             if q_due:
                 q_copy(q_due, q_due + 8, True)
-            if 1 <= s < 4:
-                k_copy(s)
+            if s in (1, 4, 8):
+                k_copy((s + 4) // 4)
             if 4 <= s:
                 finish(s - 4, 0, TB, False)
             if 3 <= s:

@@ -57,11 +57,9 @@ def tile_modelnew_kernel(tc, Q, K, V, out):
         pb0 = const.tile([P, 8, 4, P], BF16)
         pb1 = const.tile([P, 8, 4, P], BF16)
         ident = const.tile([P, P], BF16)
-        eps_t = const.tile([P, 1], F32)
 
         make_identity(nc, ident[:])
         nc.vector.memset(pb0[:].bitcast(I32), 0)
-        nc.vector.memset(eps_t[:], EPS)
 
         def load_k(g0, g1):
             nc.sync.dma_start(
@@ -76,21 +74,19 @@ def tile_modelnew_kernel(tc, Q, K, V, out):
                     in_=Q[0, h, QB * t0 : QB * t1, :].rearrange("(n q) d -> q n d", q=QB),
                 )
 
-        def load_v(first, step, count):
+        def load_v(first, count):
             nc.sync.dma_start(
-                out=v_raw[:, first : min(NV, first + step * count) : step, :, :].rearrange("p v t d -> p v (t d)"),
-                in_=V[0, 0, 256 * first : 256 * first + 256 * step * count, :].rearrange("(v p t) d -> p v (t d)", p=P, t=4),
+                out=v_raw[:, first:NV:2, :, :].rearrange("p v t d -> p v (t d)"),
+                in_=V[0, 0, 256 * first : 256 * first + 512 * count, :].rearrange("(v p t) d -> p v (t d)", p=P, t=4),
             )
 
         load_k(0, 1)
         load_q(0, 4)
         load_q(4, 16)
-        load_k(1, 2)
-        load_q(16, 24)
-        load_v(0, 2, 4)
-        load_v(1, 2, 3)
-        load_q(24, 32)
-        load_k(2, 4)
+        load_k(1, 4)
+        load_q(16, 32)
+        load_v(0, 4)
+        load_v(1, 3)
         load_q(32, 64)
 
         kt_flat = kt[:].rearrange("d l t e -> d (l t e)")
@@ -287,7 +283,9 @@ def tile_modelnew_kernel(tc, Q, K, V, out):
 
         def l_eps(b):
             le = small.tile([P, TB], F32, tag="le")
-            nc.scalar.activation(out=le[:], in_=state[("ls", b)][:], func=ACT.Identity, bias=eps_t[:, 0:1], scale=1.0)
+            nc.gpsimd.tensor_scalar(
+                out=le[:], in0=state[("ls", b)][:], scalar1=1.0, scalar2=EPS, op0=ALU.mult, op1=ALU.add
+            )
             state[("le", b)] = le
 
         def recip(b):
@@ -338,9 +336,13 @@ def tile_modelnew_kernel(tc, Q, K, V, out):
         q_tr(0, 4)
         k_copy(0)
         q_copy(0, 4, True)
-        nc.vector.memset(pb1[:].bitcast(I32), 0)
         for n in range(3):
             scores(n)
+        q_tr(4, 8)
+        q_copy(4, 8, False)
+        q_tr(8, 16)
+        nc.vector.memset(pb1[:].bitcast(I32), 0)
+        q_copy(8, 16, False)
         for s in range(NB):
             q_due = 8 * (s // 2 + 1) if (s % 2 == 0 and 2 <= s <= 12) else 0
             if 3 <= s:
@@ -350,21 +352,14 @@ def tile_modelnew_kernel(tc, Q, K, V, out):
                 neg_bias(s - 2)
             if 1 <= s:
                 row_max(s - 1)
-            if s == 1:
-                q_copy(8, 16, False)
             for i in range(TB):
                 tanh(s, i)
                 if TB * s + i + 3 < NT:
                     scores(TB * s + i + 3)
-                if s == 0 and i == 0:
-                    q_tr(4, 8)
-                    q_copy(4, 8, False)
-                if s == 0 and i == 0:
-                    q_tr(8, 16)
                 if i == 0 and q_due:
                     q_tr(q_due, q_due + 8)
-                if i == 0 and s in (1, 4, 8):
-                    k_tr((s + 4) // 4)
+                if i == 0 and 1 <= s < 4:
+                    k_tr(s)
                 if i == 2 and 4 <= s:
                     mx(s - 4, 0, TB, False)
                 if i == 2 and 3 <= s:
@@ -381,8 +376,8 @@ def tile_modelnew_kernel(tc, Q, K, V, out):
                 l_eps(s - 2)
             if q_due:
                 q_copy(q_due, q_due + 8, True)
-            if s in (1, 4, 8):
-                k_copy((s + 4) // 4)
+            if 1 <= s < 4:
+                k_copy(s)
             if 4 <= s:
                 finish(s - 4, 0, TB, False)
             if 3 <= s:

from contextlib import ExitStack

import concourse.mybir as mybir
from concourse.masks import make_identity

BF16 = mybir.dt.bfloat16
F32 = mybir.dt.float32
U32 = mybir.dt.uint32
U8 = mybir.dt.uint8
I32 = mybir.dt.int32
FP8X4 = mybir.dt.float8_e4m3fn_x4
ACT = mybir.ActivationFunctionType
ALU = mybir.AluOpType
AX = mybir.AxisListType

P = 128
H = 4
S = 2048
D = 128
WIN = 256
QB = 32
NT = S // QB
TB = 4
NB = NT // TB
NG = (WIN + QB) // 32
CW = 8 * NG
SOFTCAP = 30.0
SCALE = 1.0 / (128.0 ** 0.5)
EPS = 1e-9
FILL = -10000.0
NV = 7

FLOPS = 4 * H * D * (S * (WIN + 1) - WIN * (WIN + 1) // 2)


def tile_modelnew_kernel(tc, Q, K, V, out):
    nc = tc.nc
    with ExitStack() as ctx:
        ctx.enter_context(tc.manual_schedule())
        const = ctx.enter_context(tc.tile_pool(name="const", bufs=1))
        tbp = ctx.enter_context(tc.tile_pool(name="tbp", bufs=4))
        small = ctx.enter_context(tc.tile_pool(name="small", bufs=6))
        gp = ctx.enter_context(tc.tile_pool(name="gp", bufs=3))
        op = ctx.enter_context(tc.tile_pool(name="op", bufs=4))
        ps_s = ctx.enter_context(tc.psum_pool(name="ps_s", bufs=3))
        ps_t = ctx.enter_context(tc.psum_pool(name="ps_t", bufs=4))
        ps_o = ctx.enter_context(tc.psum_pool(name="ps_o", bufs=1))

        k_sb = const.tile([P, 4, 4, D], BF16)
        q_sb = const.tile([P, NT, D], BF16)
        v_raw = const.tile([P, NV, 4, D], BF16)
        v_grp = const.tile([P, NV, D, 4], BF16, align_bytes=64)
        v_w = const.tile([P, NV * D], U32, align_bytes=64)
        v_s = const.tile([P, NV * D], U8, align_bytes=64)
        kt = const.tile([P, S // 32, 4, 8], BF16)
        qt = const.tile([P, NT, P], BF16)
        pb0 = const.tile([P, 8, 4, P], BF16)
        pb1 = const.tile([P, 8, 4, P], BF16)
        ident = const.tile([P, P], BF16)

        make_identity(nc, ident[:])
        nc.vector.memset(pb0[:].bitcast(I32), 0)

        def load_k(g0, g1):
            nc.sync.dma_start(
                out=k_sb[:, g0:g1, :, :].rearrange("c g t d -> c g (t d)"),
                in_=K[0, 0, 512 * g0 : 512 * g1, :].rearrange("(g c t) d -> c g (t d)", c=P, t=4),
            )

        def load_q(t0, t1):
            for h in range(H):
                nc.sync.dma_start(
                    out=q_sb[h:P:H, t0:t1, :],
                    in_=Q[0, h, QB * t0 : QB * t1, :].rearrange("(n q) d -> q n d", q=QB),
                )

        def load_v(first, count):
            nc.sync.dma_start(
                out=v_raw[:, first:NV:2, :, :].rearrange("p v t d -> p v (t d)"),
                in_=V[0, 0, 256 * first : 256 * first + 512 * count, :].rearrange("(v p t) d -> p v (t d)", p=P, t=4),
            )

        load_k(0, 1)
        load_q(0, 4)
        load_q(4, 16)
        load_k(1, 4)
        load_q(16, 32)
        load_v(0, 4)
        load_v(1, 3)
        load_q(32, 64)

        kt_flat = kt[:].rearrange("d l t e -> d (l t e)")
        state = {}

        def k_tr(g):
            tp = ps_t.tile([P, 1024], BF16, tag="tp")
            for t in range(4):
                nc.tensor.transpose(tp[:, P * t : P * (t + 1)], k_sb[:, g, t, :], ident[:])
            state[("ktp", g)] = tp

        def k_copy(g):
            tp = state[("ktp", g)]
            nc.vector.tensor_copy(
                out=kt[:, 16 * g : 16 * (g + 1), :, :],
                in_=tp[:, 0:512].rearrange("d (t l e) -> d l t e", t=4, e=8),
            )

        def q_tr(n0, n1):
            tp = ps_t.tile([P, 1024], BF16, tag="tp")
            for n in range(n0, n1):
                nc.tensor.transpose(tp[:, P * (n - n0) : P * (n - n0 + 1)], q_sb[:, n, :], ident[:])
            state[("qtp", n0)] = tp

        def q_copy(n0, n1, on_scalar):
            dst = qt[:, n0:n1, :].rearrange("d n p -> d (n p)")
            src = state[("qtp", n0)][:, 0 : P * (n1 - n0)]
            if on_scalar:
                nc.scalar.copy(out=dst, in_=src)
            else:
                nc.vector.tensor_copy(out=dst, in_=src)

        def v_prep(v0, v1):
            nc.vector.tensor_copy(
                out=v_grp[:, v0:v1, :, :],
                in_=v_raw[:, v0:v1, :, :].rearrange("p v t d -> p v d t"),
            )

        def v_quant(v0, v1):
            nc.vector.quantize_mx(
                out=v_w[:, D * v0 : D * (v1)].bitcast(FP8X4),
                scales=v_s[:, D * v0 : D * v1],
                in_=v_grp[:, v0:v1, :, :].rearrange("p v d t -> p (v d t)"),
            )

        def scores(n):
            lo = max(0, 8 - n)
            bank = ps_s.tile([P, TB * D], F32, tag="sc")
            sc = bank[:, 0 : 32 * NG].rearrange("p (g e) -> p g e", e=32)
            nc.tensor.matmul(
                out=sc[:, lo:NG, :].rearrange("p g e -> p (g e)"),
                lhsT=qt[:, n, :],
                rhs=kt_flat[:, 32 * (n - 8 + lo) : 32 * (n + 1)],
                start=True,
                stop=True,
            )
            state[("sc", n)] = sc

        def tanh(b, i):
            n = TB * b + i
            lo = max(0, 8 - n)
            if i == 0:
                tb_new = tbp.tile([P, NG, TB, 32], F32, tag="tb")
                state[("tb", b)] = tb_new
            nc.scalar.activation(
                out=state[("tb", b)][:, lo:NG, i, :],
                in_=state[("sc", n)][:, lo:NG, :],
                func=ACT.Tanh,
                scale=SCALE / SOFTCAP,
            )

        def masks(b):
            tb = state[("tb", b)]
            if b >= 2:
                nc.gpsimd.affine_select(
                    out=tb[:, 0, :, :].rearrange("p i e -> p (i e)"),
                    in_=tb[:, 0, :, :].rearrange("p i e -> p (i e)"),
                    pattern=[[0, TB], [4, 4], [16, 8]],
                    compare_op=ALU.is_ge,
                    fill=FILL,
                    base=3,
                    channel_multiplier=-1,
                )
            nc.gpsimd.affine_select(
                out=tb[:, NG - 1, :, :].rearrange("p i e -> p (i e)"),
                in_=tb[:, NG - 1, :, :].rearrange("p i e -> p (i e)"),
                pattern=[[0, TB], [-4, 4], [-16, 8]],
                compare_op=ALU.is_ge,
                fill=FILL,
                base=0,
                channel_multiplier=1,
            )

        def row_max(b):
            tb = state[("tb", b)]
            mt = small.tile([P, TB], F32, tag="mt")
            nb = small.tile([P, TB], F32, tag="nb")
            if b < 2:
                for i in range(TB):
                    lo = max(0, 8 - (TB * b + i))
                    nc.vector.tensor_reduce(
                        out=mt[:, i : i + 1], in_=tb[:, lo:NG, i, :], axis=AX.XY, op=ALU.max
                    )
            else:
                nc.vector.tensor_reduce(
                    out=mt[:], in_=tb[:].rearrange("p g i e -> p i g e"), axis=AX.XY, op=ALU.max
                )
            state[("mt", b)] = mt
            state[("nb", b)] = nb

        def neg_bias(b):
            nc.scalar.mul(state[("nb", b)][:], state[("mt", b)][:], -SOFTCAP)

        def exps(b, i):
            n = TB * b + i
            j = n % 8
            lo = max(0, 8 - n)
            c0 = 8 * j if b >= 2 else 8 * j - 64
            pb = pb0 if b < 2 else pb1
            if i == 0:
                ls_new = small.tile([P, TB], F32, tag="ls")
                state[("ls", b)] = ls_new
            nc.scalar.activation(
                out=pb[:, j, :, c0 + 8 * lo : c0 + CW].rearrange("p t (g e) -> p g t e", e=8),
                in_=state[("tb", b)][:, lo:NG, i, :].rearrange("p g (t e) -> p g t e", e=8),
                func=ACT.Exp,
                scale=SOFTCAP,
                bias=state[("nb", b)][:, i : i + 1],
                accum_out=state[("ls", b)][:, i : i + 1],
            )

        def p_transposes(b, k):
            pb = pb0 if b < 2 else pb1
            tp = ps_t.tile([P, 1024], BF16, tag="tp")
            for i in range(2):
                j = (TB * b + 2 * k + i) % 8
                for t in range(4):
                    m = 4 * i + t
                    if m < 5:
                        nc.tensor.matmul(
                            out=tp[:, P * m : P * (m + 1)],
                            lhsT=pb[:, j, t, :],
                            rhs=ident[:],
                            start=True,
                            stop=True,
                        )
                    else:
                        nc.tensor.transpose(tp[:, P * m : P * (m + 1)], pb[:, j, t, :], ident[:])
            state[("tp", b, k)] = tp

        def stage_out(b, k, on_scalar):
            stg = gp.tile([P, 1024], BF16, tag="stg")
            if on_scalar:
                nc.scalar.copy(out=stg[:], in_=state[("tp", b, k)][:])
            else:
                nc.vector.tensor_copy(out=stg[:], in_=state[("tp", b, k)][:])
            state[("stg", b, k)] = stg

        def regroup(b, k):
            if ("grp", b) not in state:
                grp_new = gp.tile([P, TB, P, 4], BF16, tag="grp", align_bytes=64)
                state[("grp", b)] = grp_new
            nc.gpsimd.tensor_scalar(
                out=state[("grp", b)][:, 2 * k : 2 * k + 2, :, :],
                in0=state[("stg", b, k)][:].rearrange("c (i t p) -> c i p t", i=2, t=4),
                scalar1=1.0,
                scalar2=0.0,
                op0=ALU.mult,
                op1=ALU.add,
            )

        def copy_out(b, k, on_scalar):
            if ("grp", b) not in state:
                grp_new = gp.tile([P, TB, P, 4], BF16, tag="grp", align_bytes=64)
                state[("grp", b)] = grp_new
            src = state[("tp", b, k)][:].rearrange("c (i t p) -> c i p t", i=2, t=4)
            dst = state[("grp", b)][:, 2 * k : 2 * k + 2, :, :]
            if on_scalar:
                nc.scalar.copy(out=dst, in_=src)
            else:
                nc.vector.tensor_copy(out=dst, in_=src)

        def quantise(b, i0, i1):
            if ("pw", b) not in state:
                pw_new = gp.tile([P, TB * P], U32, tag="pw", align_bytes=64)
                psc_new = gp.tile([P, TB * P], U8, tag="psc", align_bytes=64)
                state[("pw", b)] = (pw_new, psc_new)
            pw, psc = state[("pw", b)]
            nc.vector.quantize_mx(
                out=pw[:, P * i0 : P * i1].bitcast(FP8X4),
                scales=psc[:, P * i0 : P * i1],
                in_=state[("grp", b)][:, i0:i1, :, :].rearrange("c i p t -> c (i p t)"),
            )

        def l_eps(b):
            le = small.tile([P, TB], F32, tag="le")
            nc.gpsimd.tensor_scalar(
                out=le[:], in0=state[("ls", b)][:], scalar1=1.0, scalar2=EPS, op0=ALU.mult, op1=ALU.add
            )
            state[("le", b)] = le

        def recip(b):
            rl = small.tile([P, TB], F32, tag="rl")
            nc.vector.reciprocal(out=rl[:], in_=state[("le", b)][:])
            state[("rl", b)] = rl

        def mx(b, i0, i1, spare):
            pw, psc = state[("pw", b)]
            if spare:
                ob = ps_s.tile([P, TB * D], F32, tag="sc")
            else:
                ob = ps_o.tile([P, TB * D], F32, tag="ob")
            v = max(0, b // 2 - 1)
            for i in range(i0, i1):
                nc.tensor.matmul_mx(
                    out=ob[:, D * i : D * (i + 1)],
                    lhsT=pw[:, P * i : P * (i + 1)].bitcast(FP8X4),
                    lhsT_scale=psc[:, P * i : P * (i + 1)],
                    rhs=v_w[:, D * v : D * (v + 1)].bitcast(FP8X4),
                    rhs_scale=v_s[:, D * v : D * (v + 1)],
                    start=True,
                    stop=True,
                )
            state[("ob", b, i0)] = ob

        def finish(b, i0, i1, on_scalar):
            rl = state[("rl", b)]
            ob = state[("ob", b, i0)]
            osb = op.tile([P, TB, D], F32, tag="osb")
            if on_scalar:
                for i in range(i0, i1):
                    nc.scalar.activation(out=osb[:, i, :], in_=ob[:, D * i : D * (i + 1)], func=ACT.Copy, scale=rl[:, i : i + 1])
            else:
                nc.vector.tensor_tensor(
                    out=osb[:, i0:i1, :],
                    in0=ob[:, D * i0 : D * i1].rearrange("p (i d) -> p i d", d=D),
                    in1=rl[:, i0:i1].unsqueeze(2).to_broadcast([P, i1 - i0, D]),
                    op=ALU.mult,
                )
            for h in range(H):
                nc.sync.dma_start(
                    out=out[0, h, P * b + QB * i0 : P * b + QB * i1, :].rearrange("(i q) d -> q i d", q=QB),
                    in_=osb[h:P:H, i0:i1, :],
                )

        k_tr(0)
        q_tr(0, 4)
        k_copy(0)
        q_copy(0, 4, True)
        for n in range(3):
            scores(n)
        q_tr(4, 8)
        q_copy(4, 8, False)
        q_tr(8, 16)
        nc.vector.memset(pb1[:].bitcast(I32), 0)
        q_copy(8, 16, False)
        for s in range(NB):
            q_due = 8 * (s // 2 + 1) if (s % 2 == 0 and 2 <= s <= 12) else 0
            if 3 <= s:
                regroup(s - 3, 0)

            if 2 <= s:
                neg_bias(s - 2)
            if 1 <= s:
                row_max(s - 1)
            for i in range(TB):
                tanh(s, i)
                if TB * s + i + 3 < NT:
                    scores(TB * s + i + 3)
                if i == 0 and q_due:
                    q_tr(q_due, q_due + 8)
                if i == 0 and 1 <= s < 4:
                    k_tr(s)
                if i == 2 and 4 <= s:
                    mx(s - 4, 0, TB, False)
                if i == 2 and 3 <= s:
                    copy_out(s - 3, 1, False)
                if 2 <= s:
                    exps(s - 2, i)
                    if i == 1:
                        p_transposes(s - 2, 0)
                    if i == 3:
                        p_transposes(s - 2, 1)
            masks(s)
            if 2 <= s:
                stage_out(s - 2, 0, True)
                l_eps(s - 2)
            if q_due:
                q_copy(q_due, q_due + 8, True)
            if 1 <= s < 4:
                k_copy(s)
            if 4 <= s:
                finish(s - 4, 0, TB, False)
            if 3 <= s:
                quantise(s - 3, 0, TB)
                recip(s - 3)
            if s == 2:
                v_prep(0, 4)
            if s == 3:
                v_quant(0, 4)
                v_prep(4, 6)
                v_prep(6, 7)
            if s == 4:
                v_quant(4, 6)
                v_quant(6, 7)
        regroup(NB - 3, 0)
        neg_bias(NB - 2)
        row_max(NB - 1)
        mx(NB - 4, 0, TB, False)
        for i in range(TB):
            exps(NB - 2, i)
            if i % 2 == 1:
                p_transposes(NB - 2, i // 2)
        l_eps(NB - 2)
        copy_out(NB - 3, 1, False)
        finish(NB - 4, 0, TB, False)
        quantise(NB - 3, 0, TB)
        recip(NB - 3)
        neg_bias(NB - 1)
        for i in range(TB):
            exps(NB - 1, i)
            if i % 2 == 1:
                p_transposes(NB - 1, i // 2)
        l_eps(NB - 1)
        mx(NB - 3, 0, TB, True)
        copy_out(NB - 2, 0, True)
        copy_out(NB - 2, 1, False)
        copy_out(NB - 1, 0, True)
        copy_out(NB - 1, 1, False)
        finish(NB - 3, 0, TB, True)
        quantise(NB - 2, 0, TB)
        recip(NB - 2)
        mx(NB - 2, 0, TB, True)
        quantise(NB - 1, 0, TB)
        recip(NB - 1)
        mx(NB - 1, 0, TB, False)
        finish(NB - 2, 0, TB, True)
        finish(NB - 1, 0, TB, False)
